import numpy as np
import ml_dtypes


def mxq(x, axis, fmt="e4m3"):
    dtype, down = {"e4m3": (ml_dtypes.float8_e4m3fn, 7), "e5m2": (ml_dtypes.float8_e5m2, 14)}[fmt]
    v = np.moveaxis(np.asarray(x, np.float32).astype(ml_dtypes.bfloat16).astype(np.float64), axis, -1)
    blocks = v.reshape(v.shape[:-1] + (-1, 32))
    amax = np.abs(blocks).max(-1, keepdims=True)
    byte = np.maximum(np.where(amax > 0, np.frexp(amax)[1] - 1 + 127, 0) - down, 1)
    scale = np.exp2(byte - 127.0)
    codes = (blocks / scale).astype(np.float32).astype(dtype).astype(np.float64)
    return np.moveaxis((codes * scale).reshape(v.shape), -1, axis)


WIDE = False


def mx_kscale(k):
    if not WIDE:
        return np.ones(k)
    levels = np.array([10, -10, 5, -5, 0])
    a = np.random.permutation(np.resize(levels, k // 512 * 4)).reshape(k // 512, 4)
    idx = np.arange(k)
    return np.exp2(a[idx // 512, idx % 128 // 32])


BF16 = ml_dtypes.bfloat16


def bf(x):
    return np.asarray(x, np.float32).astype(BF16)


def f64(x):
    return np.asarray(x).astype(np.float64)


E2M1 = np.array([0.0, 0.5, 1.0, 1.5, 2.0, 3.0, 4.0, 6.0, -0.0, -0.5, -1.0, -1.5, -2.0, -3.0, -4.0, -6.0])


def pack_weight(w, fmt):
    k, n = w.shape
    w = f64(bf(w)).reshape(k // 32, 32, n)
    amax = np.abs(w).max(1)
    if fmt == "e4m3":
        byte = np.frexp(amax)[1] - 1 + 127 - 7
    else:
        mant, ex = np.frexp(amax / 6.0)
        byte = np.where(mant > 0.5, ex, ex - 1) + 127
    byte = np.clip(np.where(amax > 0, byte, 1), 1, 254)
    scaled = (w * np.exp2(127.0 - byte)[:, None, :]).reshape(k, n).astype(np.float32)
    by_word = np.ascontiguousarray(scaled.reshape(k // 512, 128, 4, n).transpose(0, 1, 3, 2))
    if fmt == "e4m3":
        words = by_word.astype(ml_dtypes.float8_e4m3fn).view(np.uint8)
    else:
        c = by_word.astype(ml_dtypes.float4_e2m1fn).view(np.uint8) & 0xF
        words = c[..., 0::2] | (c[..., 1::2] << 4)
    return np.ascontiguousarray(words), np.ascontiguousarray(byte.astype(np.uint8).reshape(k // 512, 16, n))


def unpack_weight(words, scales, fmt):
    g, p, n, _ = words.shape
    if fmt == "e4m3":
        vals = np.ascontiguousarray(words).view(ml_dtypes.float8_e4m3fn).astype(np.float64)
    else:
        nib = np.empty((g, p, n, 4), np.uint8)
        nib[..., 0::2] = words & 0xF
        nib[..., 1::2] = words >> 4
        vals = E2M1[nib]
    vals = vals * np.repeat(np.exp2(scales.astype(np.float64) - 127.0), 8, axis=1)[..., None]
    return vals.transpose(0, 1, 3, 2).reshape(g * 512, n)

def pack4(w):
    words, scales = pack_weight(w, "e2m1")
    return words.reshape(words.shape[0], 128, -1), scales


def unpack4(words, scales):
    return unpack_weight(words.reshape(words.shape[0], 128, -1, 2), scales, "e2m1")


B, IN, MEM, CTX, H, G = 512, 512, 512, 1024, 4, 3


def sigmoid(v):
    return 1.0 / (1.0 + np.exp(-v))


def setup_inputs():
    s = mx_kscale(IN)
    w = np.random.standard_normal((MEM, MEM + IN)) / np.sqrt(MEM + IN)
    w[:, MEM:] = w[:, MEM:] / s
    input_tensor = bf(np.random.standard_normal((B, IN)) * s)
    previous_memory = bf(np.random.standard_normal((B, MEM)))
    words, scales = pack4(np.ascontiguousarray(w.T))
    return {"input_tensor": input_tensor,
            "previous_memory": previous_memory,
            "fg_w_words": words,
            "fg_w_scales": scales,
            "fg_b": bf(np.random.standard_normal(MEM) * 0.3)}


def reference(input_tensor, previous_memory, fg_w_words, fg_w_scales, fg_b):
    m = f64(previous_memory)
    forget_in = np.concatenate([m, f64(input_tensor)], axis=-1)
    fgate = sigmoid((mxq(forget_in, 1, "e4m3") @ unpack4(fg_w_words, fg_w_scales)) + f64(fg_b))
    return m * fgate

@@ -1,0 +1,117 @@
+import concourse.mybir as mybir
+from concourse.masks import make_identity
+
+F32 = mybir.dt.float32
+BF16 = mybir.dt.bfloat16
+I32 = mybir.dt.int32
+U32 = mybir.dt.uint32
+U8 = mybir.dt.uint8
+FP8X4 = mybir.dt.float8_e4m3fn_x4
+FP4X4 = mybir.dt.float4_e2m1fn_x4
+ADD = mybir.AluOpType.add
+MULT = mybir.AluOpType.mult
+SIGMOID = mybir.ActivationFunctionType.Sigmoid
+
+P = 128
+PACK = 4
+PAIR = 2
+ROWS = 512
+COLS = 512
+PASSES = 2
+K_PASS = P * PACK
+ROW_TILES = ROWS // P
+TILES_PER_LOAD = 2
+LOADS = ROW_TILES // TILES_PER_LOAD
+QUADRANTS = 4
+
+FLOPS = 2 * ROWS * PASSES * K_PASS * COLS
+
+
+def tile_dynamicmemorycell_pa_s_kernel(
+    tc, input_tensor, previous_memory, fg_w_words, fg_w_scales, fg_b, out
+):
+    nc = tc.nc
+    with tc.tile_pool(name="keep", bufs=1) as keep, tc.tile_pool(
+        name="work", bufs=ROW_TILES
+    ) as work, tc.psum_pool(name="psum_t", bufs=2) as psum_t, tc.psum_pool(
+        name="psum_z", bufs=ROW_TILES
+    ) as psum_z, tc.psum_pool(name="psum_b", bufs=1) as psum_b:
+        w_planes = keep.tile([P, PASSES, COLS], U8, align_bytes=64)
+        nc.vector.memset(w_planes[:].bitcast(I32), 0)
+        bias_rows = keep.tile([P, COLS], BF16)
+        nc.vector.memset(bias_rows[:].bitcast(I32), 0)
+        ones = keep.tile([P, P], BF16)
+        nc.vector.memset(ones[:], 1.0)
+        warm = keep.tile([P, 1], F32)
+        nc.vector.memset(warm[:], 0.0)
+        nc.scalar.activation(out=warm[:], in_=warm[:], func=SIGMOID)
+
+        nc.gpsimd.dma_start(out=bias_rows[0:1, :], in_=fg_b.rearrange("(o n) -> o n", o=1))
+        ident = keep.tile([P, P], F32)
+        make_identity(nc, ident[:])
+
+        sources = (previous_memory, input_tensor)
+        x_rows = [
+            [keep.tile([P, TILES_PER_LOAD, K_PASS], BF16, name="x_g%d_h%d" % (g, h)) for h in range(LOADS)]
+            for g in range(PASSES)
+        ]
+        w_words = keep.tile([P, PASSES, 2 * COLS], U8, align_bytes=64)
+
+        def load_rows(h):
+            for g in range(PASSES):
+                by_tile = sources[g].rearrange("(i p) k -> p i k", p=P)
+                nc.sync.dma_start(
+                    out=x_rows[g][h][:], in_=by_tile[:, h * TILES_PER_LOAD : (h + 1) * TILES_PER_LOAD, :]
+                )
+
+        load_rows(0)
+        scale_rows = fg_w_scales.bitcast(I32).rearrange("g q n -> q g n")
+        for r in range(PACK):
+            nc.sync.dma_start(
+                out=w_planes[r:P:32, :, :].bitcast(I32), in_=scale_rows[r : PACK * QUADRANTS : PACK, :, :]
+            )
+        nc.sync.dma_start(out=w_words[:].bitcast(I32), in_=fg_w_words.bitcast(I32).rearrange("g p w -> p g w"))
+        load_rows(1)
+
+        bias_ps = psum_b.tile([P, COLS], F32)
+        nc.tensor.matmul(out=bias_ps[:], lhsT=ones[:], rhs=bias_rows[:], start=True, stop=True)
+        bias_all = keep.tile([P, COLS], F32)
+        nc.scalar.copy(out=bias_all[:], in_=bias_ps[:])
+
+        for i in range(ROW_TILES):
+            h, j = divmod(i, TILES_PER_LOAD)
+
+            turned = psum_t.tile([P, PASSES, PAIR, P], F32)
+            for g in range(PASSES):
+                row_words = x_rows[g][h][:, j, :].bitcast(F32)
+                for u in range(PAIR):
+                    nc.tensor.transpose(turned[:, g, u, :], row_words[:, u : K_PASS // PAIR : PAIR], ident[:])
+            grouped = work.tile([P, PASSES, P, PACK], BF16, align_bytes=64)
+            nc.scalar.copy(out=grouped[:].bitcast(F32), in_=turned[:].rearrange("p g u b -> p g b u"))
+            x_codes = work.tile([P, PASSES, P], U32, align_bytes=64)
+            x_planes = work.tile([P, PASSES, P], U8, align_bytes=64)
+            nc.vector.quantize_mx(
+                out=x_codes[:].rearrange("p g b -> p (g b)").bitcast(FP8X4),
+                scales=x_planes[:].rearrange("p g b -> p (g b)"),
+                in_=grouped[:].rearrange("p g b t -> p (g b t)"),
+            )
+
+            z = psum_z.tile([P, COLS], F32)
+            for g in range(PASSES):
+                nc.tensor.matmul_mx(
+                    out=z[:],
+                    lhsT=x_codes[:, g, :].bitcast(FP8X4),
+                    lhsT_scale=x_planes[:, g, :],
+                    rhs=w_words[:, g, :].bitcast(FP4X4),
+                    rhs_scale=w_planes[:, g, :],
+                    start=(g == 0),
+                    stop=(g == PASSES - 1),
+                )
+
+            z_biased = work.tile([P, COLS], F32)
+            nc.vector.tensor_tensor(out=z_biased[:], in0=z[:], in1=bias_all[:], op=ADD)
+            gate = work.tile([P, COLS], F32)
+            nc.scalar.activation(out=gate[:], in_=z_biased[:], func=SIGMOID)
+            result = work.tile([P, COLS], F32)
+            nc.vector.tensor_tensor(out=result[:], in0=gate[:], in1=x_rows[0][h][:, j, :], op=MULT)
+            nc.sync.dma_start(out=out[i * P : (i + 1) * P, :], in_=result[:])

@@ -33,22 +33,22 @@ def tile_dynamicmemorycell_pa_s_kernel(
     nc = tc.nc
     with tc.tile_pool(name="keep", bufs=1) as keep, tc.tile_pool(
         name="work", bufs=ROW_TILES
-    ) as work, tc.psum_pool(name="psum_t", bufs=2) as psum_t, tc.psum_pool(
+    ) as work, tc.psum_pool(name="psum_t", bufs=3) as psum_t, tc.psum_pool(
         name="psum_z", bufs=ROW_TILES
-    ) as psum_z, tc.psum_pool(name="psum_b", bufs=1) as psum_b:
-        w_planes = keep.tile([P, PASSES, COLS], U8, align_bytes=64)
-        nc.vector.memset(w_planes[:].bitcast(I32), 0)
+    ) as psum_z, tc.psum_pool(name="psum_b", bufs=1) as psum_b, tc.manual_schedule():
         bias_rows = keep.tile([P, COLS], BF16)
         nc.vector.memset(bias_rows[:].bitcast(I32), 0)
-        ones = keep.tile([P, P], BF16)
-        nc.vector.memset(ones[:], 1.0)
+        nc.scalar.dma_start(out=bias_rows[0:1, :], in_=fg_b.rearrange("(o n) -> o n", o=1))
+        ident = keep.tile([P, P], F32)
+        nc.vector.memset(ident[:], 0.0)
+        make_identity(nc, ident[:], nomemset=True)
+        w_planes = keep.tile([P, PASSES, COLS], U8, align_bytes=64)
+        nc.vector.memset(w_planes[:].bitcast(I32), 0)
         warm = keep.tile([P, 1], F32)
         nc.vector.memset(warm[:], 0.0)
         nc.scalar.activation(out=warm[:], in_=warm[:], func=SIGMOID)
-
-        nc.gpsimd.dma_start(out=bias_rows[0:1, :], in_=fg_b.rearrange("(o n) -> o n", o=1))
-        ident = keep.tile([P, P], F32)
-        make_identity(nc, ident[:])
+        ones = keep.tile([P, P], BF16)
+        nc.vector.memset(ones[:], 1.0)
 
         sources = (previous_memory, input_tensor)
         x_rows = [
@@ -78,28 +78,33 @@ def tile_dynamicmemorycell_pa_s_kernel(
         bias_all = keep.tile([P, COLS], F32)
         nc.scalar.copy(out=bias_all[:], in_=bias_ps[:])
 
-        for i in range(ROW_TILES):
-            h, j = divmod(i, TILES_PER_LOAD)
+        grouped, z, gate = {}, {}, {}
 
+        def memory_rows(i):
+            h, j = divmod(i, TILES_PER_LOAD)
+            return [x_rows[g][h][:, j, :] for g in range(PASSES)]
+
+        def turn(i):
             turned = psum_t.tile([P, PASSES, PAIR, P], F32)
             for g in range(PASSES):
-                row_words = x_rows[g][h][:, j, :].bitcast(F32)
+                row_words = memory_rows(i)[g].bitcast(F32)
                 for u in range(PAIR):
                     nc.tensor.transpose(turned[:, g, u, :], row_words[:, u : K_PASS // PAIR : PAIR], ident[:])
-            grouped = work.tile([P, PASSES, P, PACK], BF16, align_bytes=64)
-            nc.scalar.copy(out=grouped[:].bitcast(F32), in_=turned[:].rearrange("p g u b -> p g b u"))
+            grouped[i] = work.tile([P, PASSES, P, PACK], BF16, align_bytes=64, name="grouped")
+            nc.scalar.copy(out=grouped[i][:].bitcast(F32), in_=turned[:].rearrange("p g u b -> p g b u"))
+
+        def quantise_and_multiply(i):
             x_codes = work.tile([P, PASSES, P], U32, align_bytes=64)
             x_planes = work.tile([P, PASSES, P], U8, align_bytes=64)
             nc.vector.quantize_mx(
                 out=x_codes[:].rearrange("p g b -> p (g b)").bitcast(FP8X4),
                 scales=x_planes[:].rearrange("p g b -> p (g b)"),
-                in_=grouped[:].rearrange("p g b t -> p (g b t)"),
+                in_=grouped[i][:].rearrange("p g b t -> p (g b t)"),
             )
-
-            z = psum_z.tile([P, COLS], F32)
+            z[i] = psum_z.tile([P, COLS], F32, name="z")
             for g in range(PASSES):
                 nc.tensor.matmul_mx(
-                    out=z[:],
+                    out=z[i][:],
                     lhsT=x_codes[:, g, :].bitcast(FP8X4),
                     lhsT_scale=x_planes[:, g, :],
                     rhs=w_words[:, g, :].bitcast(FP4X4),
@@ -108,10 +113,19 @@ def tile_dynamicmemorycell_pa_s_kernel(
                     stop=(g == PASSES - 1),
                 )
 
+        def squash(i):
             z_biased = work.tile([P, COLS], F32)
-            nc.vector.tensor_tensor(out=z_biased[:], in0=z[:], in1=bias_all[:], op=ADD)
-            gate = work.tile([P, COLS], F32)
-            nc.scalar.activation(out=gate[:], in_=z_biased[:], func=SIGMOID)
+            nc.vector.tensor_tensor(out=z_biased[:], in0=z[i][:], in1=bias_all[:], op=ADD)
+            gate[i] = work.tile([P, COLS], F32, name="gate")
+            nc.scalar.activation(out=gate[i][:], in_=z_biased[:], func=SIGMOID)
+
+        def finish(i):
             result = work.tile([P, COLS], F32)
-            nc.vector.tensor_tensor(out=result[:], in0=gate[:], in1=x_rows[0][h][:, j, :], op=MULT)
+            nc.vector.tensor_tensor(out=result[:], in0=gate[i][:], in1=memory_rows(i)[0], op=MULT)
             nc.sync.dma_start(out=out[i * P : (i + 1) * P, :], in_=result[:])
+
+        stages = (turn, quantise_and_multiply, squash, finish)
+        for step in range(ROW_TILES + len(stages) - 1):
+            for lag, stage in enumerate(stages):
+                if 0 <= step - lag < ROW_TILES:
+                    stage(step - lag)

@@ -20,9 +20,8 @@ COLS = 512
 PASSES = 2
 K_PASS = P * PACK
 ROW_TILES = ROWS // P
-TILES_PER_LOAD = 2
-LOADS = ROW_TILES // TILES_PER_LOAD
 QUADRANTS = 4
+FINISH_LAG = 2
 
 FLOPS = 2 * ROWS * PASSES * K_PASS * COLS
 
@@ -36,82 +35,81 @@ def tile_dynamicmemorycell_pa_s_kernel(
     ) as work, tc.psum_pool(name="psum_t", bufs=3) as psum_t, tc.psum_pool(
         name="psum_z", bufs=ROW_TILES
     ) as psum_z, tc.psum_pool(name="psum_b", bufs=1) as psum_b, tc.manual_schedule():
-        bias_rows = keep.tile([P, COLS], BF16)
-        nc.vector.memset(bias_rows[:].bitcast(I32), 0)
-        nc.scalar.dma_start(out=bias_rows[0:1, :], in_=fg_b.rearrange("(o n) -> o n", o=1))
+
         ident = keep.tile([P, P], F32)
         nc.vector.memset(ident[:], 0.0)
         make_identity(nc, ident[:], nomemset=True)
         w_planes = keep.tile([P, PASSES, COLS], U8, align_bytes=64)
         nc.vector.memset(w_planes[:].bitcast(I32), 0)
+        bias_rows = keep.tile([P, COLS], BF16)
+        nc.vector.memset(bias_rows[:].bitcast(I32), 0)
+        nc.gpsimd.dma_start(out=bias_rows[0:1, :], in_=fg_b.rearrange("(o n) -> o n", o=1))
+        ones = keep.tile([P, P], BF16)
+        nc.vector.memset(ones[:], 1.0)
         warm = keep.tile([P, 1], F32)
         nc.vector.memset(warm[:], 0.0)
         nc.scalar.activation(out=warm[:], in_=warm[:], func=SIGMOID)
-        ones = keep.tile([P, P], BF16)
-        nc.vector.memset(ones[:], 1.0)
 
-        sources = (previous_memory, input_tensor)
-        x_rows = [
-            [keep.tile([P, TILES_PER_LOAD, K_PASS], BF16, name="x_g%d_h%d" % (g, h)) for h in range(LOADS)]
-            for g in range(PASSES)
+        by_tile = [
+            source.rearrange("(i p) k -> p i k", p=P) for source in (previous_memory, input_tensor)
         ]
-        w_words = keep.tile([P, PASSES, 2 * COLS], U8, align_bytes=64)
+        x_rows = {}
 
-        def load_rows(h):
+        def load_rows(first, count):
             for g in range(PASSES):
-                by_tile = sources[g].rearrange("(i p) k -> p i k", p=P)
-                nc.sync.dma_start(
-                    out=x_rows[g][h][:], in_=by_tile[:, h * TILES_PER_LOAD : (h + 1) * TILES_PER_LOAD, :]
-                )
+                loaded = keep.tile([P, count, K_PASS], BF16, name="x_g%d_i%d" % (g, first))
+                nc.sync.dma_start(out=loaded[:], in_=by_tile[g][:, first : first + count, :])
+                for j in range(count):
+                    x_rows[(g, first + j)] = loaded[:, j, :]
 
-        load_rows(0)
+        load_rows(0, 1)
+        load_rows(1, 1)
+        load_rows(2, 2)
+        w_words = keep.tile([P, PASSES, 2 * COLS], U8, align_bytes=64)
+        nc.sync.dma_start(out=w_words[:].bitcast(I32), in_=fg_w_words.bitcast(I32).rearrange("g p w -> p g w"))
         scale_rows = fg_w_scales.bitcast(I32).rearrange("g q n -> q g n")
         for r in range(PACK):
             nc.sync.dma_start(
                 out=w_planes[r:P:32, :, :].bitcast(I32), in_=scale_rows[r : PACK * QUADRANTS : PACK, :, :]
             )
-        nc.sync.dma_start(out=w_words[:].bitcast(I32), in_=fg_w_words.bitcast(I32).rearrange("g p w -> p g w"))
-        load_rows(1)
+
+        x_codes, x_planes = {}, {}
+        for i in range(ROW_TILES):
+            turned = psum_t.tile([P, PASSES, PAIR, P], F32)
+            for g in range(PASSES):
+                row_words = x_rows[(g, i)].bitcast(F32)
+                for u in range(PAIR):
+                    nc.tensor.transpose(turned[:, g, u, :], row_words[:, u : K_PASS // PAIR : PAIR], ident[:])
+            grouped = work.tile([P, PASSES, P, PACK], BF16, align_bytes=64)
+            nc.scalar.copy(out=grouped[:].bitcast(F32), in_=turned[:].rearrange("p g u b -> p g b u"))
+            x_codes[i] = work.tile([P, PASSES, P], U32, align_bytes=64, name="x_codes")
+            x_planes[i] = work.tile([P, PASSES, P], U8, align_bytes=64, name="x_planes")
+            nc.vector.quantize_mx(
+                out=x_codes[i][:].rearrange("p g b -> p (g b)").bitcast(FP8X4),
+                scales=x_planes[i][:].rearrange("p g b -> p (g b)"),
+                in_=grouped[:].rearrange("p g b t -> p (g b t)"),
+            )
 
         bias_ps = psum_b.tile([P, COLS], F32)
         nc.tensor.matmul(out=bias_ps[:], lhsT=ones[:], rhs=bias_rows[:], start=True, stop=True)
         bias_all = keep.tile([P, COLS], F32)
         nc.scalar.copy(out=bias_all[:], in_=bias_ps[:])
 
-        grouped, z, gate = {}, {}, {}
-
-        def memory_rows(i):
-            h, j = divmod(i, TILES_PER_LOAD)
-            return [x_rows[g][h][:, j, :] for g in range(PASSES)]
-
-        def turn(i):
-            turned = psum_t.tile([P, PASSES, PAIR, P], F32)
-            for g in range(PASSES):
-                row_words = memory_rows(i)[g].bitcast(F32)
-                for u in range(PAIR):
-                    nc.tensor.transpose(turned[:, g, u, :], row_words[:, u : K_PASS // PAIR : PAIR], ident[:])
-            grouped[i] = work.tile([P, PASSES, P, PACK], BF16, align_bytes=64, name="grouped")
-            nc.scalar.copy(out=grouped[i][:].bitcast(F32), in_=turned[:].rearrange("p g u b -> p g b u"))
-
-        def quantise_and_multiply(i):
-            x_codes = work.tile([P, PASSES, P], U32, align_bytes=64)
-            x_planes = work.tile([P, PASSES, P], U8, align_bytes=64)
-            nc.vector.quantize_mx(
-                out=x_codes[:].rearrange("p g b -> p (g b)").bitcast(FP8X4),
-                scales=x_planes[:].rearrange("p g b -> p (g b)"),
-                in_=grouped[i][:].rearrange("p g b t -> p (g b t)"),
-            )
+        z = {}
+        for i in range(ROW_TILES):
             z[i] = psum_z.tile([P, COLS], F32, name="z")
             for g in range(PASSES):
                 nc.tensor.matmul_mx(
                     out=z[i][:],
-                    lhsT=x_codes[:, g, :].bitcast(FP8X4),
-                    lhsT_scale=x_planes[:, g, :],
+                    lhsT=x_codes[i][:, g, :].bitcast(FP8X4),
+                    lhsT_scale=x_planes[i][:, g, :],
                     rhs=w_words[:, g, :].bitcast(FP4X4),
                     rhs_scale=w_planes[:, g, :],
                     start=(g == 0),
                     stop=(g == PASSES - 1),
                 )
+
+        gate = {}
 
         def squash(i):
             z_biased = work.tile([P, COLS], F32)
@@ -121,11 +119,11 @@ def tile_dynamicmemorycell_pa_s_kernel(
 
         def finish(i):
             result = work.tile([P, COLS], F32)
-            nc.vector.tensor_tensor(out=result[:], in0=gate[i][:], in1=memory_rows(i)[0], op=MULT)
+            nc.vector.tensor_tensor(out=result[:], in0=gate[i][:], in1=x_rows[(0, i)], op=MULT)
             nc.sync.dma_start(out=out[i * P : (i + 1) * P, :], in_=result[:])
 
-        stages = (turn, quantise_and_multiply, squash, finish)
-        for step in range(ROW_TILES + len(stages) - 1):
-            for lag, stage in enumerate(stages):
-                if 0 <= step - lag < ROW_TILES:
-                    stage(step - lag)
+        for step in range(ROW_TILES + FINISH_LAG):
+            if step < ROW_TILES:
+                squash(step)
+            if step >= FINISH_LAG:
+                finish(step - FINISH_LAG)

@@ -22,6 +22,8 @@ K_PASS = P * PACK
 ROW_TILES = ROWS // P
 QUADRANTS = 4
 FINISH_LAG = 2
+WARM_UP = 4
+KEEP_UP = 1
 
 FLOPS = 2 * ROWS * PASSES * K_PASS * COLS
 
@@ -32,7 +34,7 @@ def tile_dynamicmemorycell_pa_s_kernel(
     nc = tc.nc
     with tc.tile_pool(name="keep", bufs=1) as keep, tc.tile_pool(
         name="work", bufs=ROW_TILES
-    ) as work, tc.psum_pool(name="psum_t", bufs=3) as psum_t, tc.psum_pool(
+    ) as work, tc.psum_pool(name="psum_t", bufs=2) as psum_t, tc.psum_pool(
         name="psum_z", bufs=ROW_TILES
     ) as psum_z, tc.psum_pool(name="psum_b", bufs=1) as psum_b, tc.manual_schedule():
 
@@ -73,6 +75,14 @@ def tile_dynamicmemorycell_pa_s_kernel(
                 out=w_planes[r:P:32, :, :].bitcast(I32), in_=scale_rows[r : PACK * QUADRANTS : PACK, :, :]
             )
 
+        idle_ps = psum_b.tile([P, P], F32)
+
+        def keep_clock_up(count):
+            for n in range(count):
+                nc.tensor.matmul(out=idle_ps[:], lhsT=ident[:], rhs=ident[:], start=(n == 0), stop=(n == count - 1))
+
+        keep_clock_up(WARM_UP)
+
         x_codes, x_planes = {}, {}
         for i in range(ROW_TILES):
             turned = psum_t.tile([P, PASSES, PAIR, P], F32)
@@ -80,6 +90,7 @@ def tile_dynamicmemorycell_pa_s_kernel(
                 row_words = x_rows[(g, i)].bitcast(F32)
                 for u in range(PAIR):
                     nc.tensor.transpose(turned[:, g, u, :], row_words[:, u : K_PASS // PAIR : PAIR], ident[:])
+            keep_clock_up(KEEP_UP)
             grouped = work.tile([P, PASSES, P, PACK], BF16, align_bytes=64)
             nc.scalar.copy(out=grouped[:].bitcast(F32), in_=turned[:].rearrange("p g u b -> p g b u"))
             x_codes[i] = work.tile([P, PASSES, P], U32, align_bytes=64, name="x_codes")

@@ -21,9 +21,7 @@ PASSES = 2
 K_PASS = P * PACK
 ROW_TILES = ROWS // P
 QUADRANTS = 4
-FINISH_LAG = 2
-WARM_UP = 4
-KEEP_UP = 1
+WARM_UP = 3
 
 FLOPS = 2 * ROWS * PASSES * K_PASS * COLS
 
@@ -33,94 +31,100 @@ def tile_dynamicmemorycell_pa_s_kernel(
 ):
     nc = tc.nc
     with tc.tile_pool(name="keep", bufs=1) as keep, tc.tile_pool(
-        name="work", bufs=ROW_TILES
-    ) as work, tc.psum_pool(name="psum_t", bufs=2) as psum_t, tc.psum_pool(
-        name="psum_z", bufs=ROW_TILES
+        name="work", bufs=ROW_TILES * PASSES
+    ) as work, tc.psum_pool(name="psum_t", bufs=2 * PASSES) as psum_t, tc.psum_pool(
+        name="psum_z", bufs=ROW_TILES - 1
     ) as psum_z, tc.psum_pool(name="psum_b", bufs=1) as psum_b, tc.manual_schedule():
+
+        warm_operand = keep.tile([P, P], F32)
+        nc.vector.memset(warm_operand[:], 0.0)
+        bias_rows = keep.tile([P, COLS], BF16)
+        nc.vector.memset(bias_rows[:].bitcast(I32), 0)
+        nc.scalar.dma_start(out=bias_rows[0:1, :], in_=fg_b.rearrange("(o n) -> o n", o=1))
 
         ident = keep.tile([P, P], F32)
         nc.vector.memset(ident[:], 0.0)
         make_identity(nc, ident[:], nomemset=True)
+
+        by_tile = [
+            source.rearrange("(p i) k -> p i k", i=ROW_TILES) for source in (previous_memory, input_tensor)
+        ]
+        out_by_tile = out.rearrange("(p i) n -> p i n", i=ROW_TILES)
+        x_rows = {}
+
+        def load_rows(g, first, count):
+            loaded = keep.tile([P, count, K_PASS], BF16, name="x_g%d_i%d" % (g, first))
+            nc.sync.dma_start(out=loaded[:], in_=by_tile[g][:, first : first + count, :])
+            for j in range(count):
+                x_rows[(g, first + j)] = loaded[:, j, :]
+
+        load_rows(0, 0, 1)
+        load_rows(1, 0, 1)
         w_planes = keep.tile([P, PASSES, COLS], U8, align_bytes=64)
         nc.vector.memset(w_planes[:].bitcast(I32), 0)
-        bias_rows = keep.tile([P, COLS], BF16)
-        nc.vector.memset(bias_rows[:].bitcast(I32), 0)
-        nc.gpsimd.dma_start(out=bias_rows[0:1, :], in_=fg_b.rearrange("(o n) -> o n", o=1))
+        scale_rows = fg_w_scales.bitcast(I32).rearrange("g q n -> q g n")
+
+        def load_scales(r):
+            nc.sync.dma_start(
+                out=w_planes[r:P:32, :, :].bitcast(I32), in_=scale_rows[r : PACK * QUADRANTS : PACK, :, :]
+            )
+
+        load_rows(0, 1, ROW_TILES - 1)
+        load_rows(1, 1, ROW_TILES - 1)
+        for r in range(PACK // 2):
+            load_scales(r)
+        w_words = keep.tile([P, PASSES, 2 * COLS], U8, align_bytes=64)
+        nc.sync.dma_start(out=w_words[:].bitcast(I32), in_=fg_w_words.bitcast(I32).rearrange("g p w -> p g w"))
+        for r in range(PACK // 2, PACK):
+            load_scales(r)
+
         ones = keep.tile([P, P], BF16)
         nc.vector.memset(ones[:], 1.0)
         warm = keep.tile([P, 1], F32)
         nc.vector.memset(warm[:], 0.0)
         nc.scalar.activation(out=warm[:], in_=warm[:], func=SIGMOID)
 
-        by_tile = [
-            source.rearrange("(i p) k -> p i k", p=P) for source in (previous_memory, input_tensor)
-        ]
-        x_rows = {}
-
-        def load_rows(first, count):
-            for g in range(PASSES):
-                loaded = keep.tile([P, count, K_PASS], BF16, name="x_g%d_i%d" % (g, first))
-                nc.sync.dma_start(out=loaded[:], in_=by_tile[g][:, first : first + count, :])
-                for j in range(count):
-                    x_rows[(g, first + j)] = loaded[:, j, :]
-
-        load_rows(0, 1)
-        load_rows(1, 1)
-        load_rows(2, 2)
-        w_words = keep.tile([P, PASSES, 2 * COLS], U8, align_bytes=64)
-        nc.sync.dma_start(out=w_words[:].bitcast(I32), in_=fg_w_words.bitcast(I32).rearrange("g p w -> p g w"))
-        scale_rows = fg_w_scales.bitcast(I32).rearrange("g q n -> q g n")
-        for r in range(PACK):
-            nc.sync.dma_start(
-                out=w_planes[r:P:32, :, :].bitcast(I32), in_=scale_rows[r : PACK * QUADRANTS : PACK, :, :]
+        idle_ps = psum_z.tile([P, P], F32, name="z")
+        for n in range(WARM_UP):
+            nc.tensor.matmul(
+                out=idle_ps[:], lhsT=warm_operand[:], rhs=warm_operand[:], start=(n == 0), stop=(n == WARM_UP - 1)
             )
 
-        idle_ps = psum_b.tile([P, P], F32)
+        turned, grouped, x_codes, x_planes, z, gate = {}, {}, {}, {}, {}, {}
 
-        def keep_clock_up(count):
-            for n in range(count):
-                nc.tensor.matmul(out=idle_ps[:], lhsT=ident[:], rhs=ident[:], start=(n == 0), stop=(n == count - 1))
+        def turn(i, g):
+            turned[(i, g)] = psum_t.tile([P, PAIR, P], F32, name="turned")
+            row_words = x_rows[(g, i)].bitcast(F32)
+            for u in range(PAIR):
+                nc.tensor.transpose(turned[(i, g)][:, u, :], row_words[:, u : K_PASS // PAIR : PAIR], ident[:])
 
-        keep_clock_up(WARM_UP)
+        def group(i, g):
+            grouped[(i, g)] = work.tile([P, P, PACK], BF16, align_bytes=64, name="grouped")
+            nc.scalar.copy(
+                out=grouped[(i, g)][:].bitcast(F32), in_=turned[(i, g)][:].rearrange("p u b -> p b u")
+            )
 
-        x_codes, x_planes = {}, {}
-        for i in range(ROW_TILES):
-            turned = psum_t.tile([P, PASSES, PAIR, P], F32)
-            for g in range(PASSES):
-                row_words = x_rows[(g, i)].bitcast(F32)
-                for u in range(PAIR):
-                    nc.tensor.transpose(turned[:, g, u, :], row_words[:, u : K_PASS // PAIR : PAIR], ident[:])
-            keep_clock_up(KEEP_UP)
-            grouped = work.tile([P, PASSES, P, PACK], BF16, align_bytes=64)
-            nc.scalar.copy(out=grouped[:].bitcast(F32), in_=turned[:].rearrange("p g u b -> p g b u"))
-            x_codes[i] = work.tile([P, PASSES, P], U32, align_bytes=64, name="x_codes")
-            x_planes[i] = work.tile([P, PASSES, P], U8, align_bytes=64, name="x_planes")
+        def quantise(i, g):
+            x_codes[(i, g)] = work.tile([P, P], U32, align_bytes=64, name="x_codes")
+            x_planes[(i, g)] = work.tile([P, P], U8, align_bytes=64, name="x_planes")
             nc.vector.quantize_mx(
-                out=x_codes[i][:].rearrange("p g b -> p (g b)").bitcast(FP8X4),
-                scales=x_planes[i][:].rearrange("p g b -> p (g b)"),
-                in_=grouped[:].rearrange("p g b t -> p (g b t)"),
+                out=x_codes[(i, g)][:].bitcast(FP8X4),
+                scales=x_planes[(i, g)][:],
+                in_=grouped[(i, g)][:].rearrange("p b t -> p (b t)"),
             )
 
-        bias_ps = psum_b.tile([P, COLS], F32)
-        nc.tensor.matmul(out=bias_ps[:], lhsT=ones[:], rhs=bias_rows[:], start=True, stop=True)
-        bias_all = keep.tile([P, COLS], F32)
-        nc.scalar.copy(out=bias_all[:], in_=bias_ps[:])
-
-        z = {}
-        for i in range(ROW_TILES):
+        def multiply(i):
             z[i] = psum_z.tile([P, COLS], F32, name="z")
             for g in range(PASSES):
                 nc.tensor.matmul_mx(
                     out=z[i][:],
-                    lhsT=x_codes[i][:, g, :].bitcast(FP8X4),
-                    lhsT_scale=x_planes[i][:, g, :],
+                    lhsT=x_codes[(i, g)][:].bitcast(FP8X4),
+                    lhsT_scale=x_planes[(i, g)][:],
                     rhs=w_words[:, g, :].bitcast(FP4X4),
                     rhs_scale=w_planes[:, g, :],
                     start=(g == 0),
                     stop=(g == PASSES - 1),
                 )
-
-        gate = {}
 
         def squash(i):
             z_biased = work.tile([P, COLS], F32)
@@ -131,10 +135,38 @@ def tile_dynamicmemorycell_pa_s_kernel(
         def finish(i):
             result = work.tile([P, COLS], F32)
             nc.vector.tensor_tensor(out=result[:], in0=gate[i][:], in1=x_rows[(0, i)], op=MULT)
-            nc.sync.dma_start(out=out[i * P : (i + 1) * P, :], in_=result[:])
+            nc.sync.dma_start(out=out_by_tile[:, i, :], in_=result[:])
 
-        for step in range(ROW_TILES + FINISH_LAG):
-            if step < ROW_TILES:
-                squash(step)
-            if step >= FINISH_LAG:
-                finish(step - FINISH_LAG)
+        def prepare(i):
+            for g in range(PASSES):
+                turn(i, g)
+                group(i, g)
+
+        prepare(0)
+        prepare(1)
+        for g in range(PASSES):
+            quantise(0, g)
+        bias_ps = psum_b.tile([P, COLS], BF16)
+        nc.tensor.matmul(out=bias_ps[:], lhsT=ones[:], rhs=bias_rows[:], start=True, stop=True)
+        bias_all = keep.tile([P, COLS], BF16)
+        nc.vector.tensor_copy(out=bias_all[:], in_=bias_ps[:])
+        prepare(2)
+        for g in range(PASSES):
+            quantise(1, g)
+        multiply(0)
+        prepare(3)
+        squash(0)
+        multiply(1)
+        for g in range(PASSES):
+            quantise(2, g)
+        squash(1)
+        multiply(2)
+        for g in range(PASSES):
+            quantise(3, g)
+        finish(0)
+        squash(2)
+        multiply(3)
+        finish(1)
+        squash(3)
+        finish(2)
+        finish(3)

@@ -36,15 +36,16 @@ def tile_dynamicmemorycell_pa_s_kernel(
         name="psum_z", bufs=ROW_TILES - 1
     ) as psum_z, tc.psum_pool(name="psum_b", bufs=1) as psum_b, tc.manual_schedule():
 
+        w_planes = keep.tile([P, PASSES, COLS], U8, align_bytes=64)
+        nc.vector.memset(w_planes[:].bitcast(I32), 0)
         warm_operand = keep.tile([P, P], F32)
         nc.vector.memset(warm_operand[:], 0.0)
-        bias_rows = keep.tile([P, COLS], BF16)
-        nc.vector.memset(bias_rows[:].bitcast(I32), 0)
-        nc.scalar.dma_start(out=bias_rows[0:1, :], in_=fg_b.rearrange("(o n) -> o n", o=1))
-
         ident = keep.tile([P, P], F32)
         nc.vector.memset(ident[:], 0.0)
         make_identity(nc, ident[:], nomemset=True)
+        bias_rows = keep.tile([P, COLS], BF16)
+        nc.vector.memset(bias_rows[:].bitcast(I32), 0)
+        nc.gpsimd.dma_start(out=bias_rows[0:1, :], in_=fg_b.rearrange("(o n) -> o n", o=1))
 
         by_tile = [
             source.rearrange("(p i) k -> p i k", i=ROW_TILES) for source in (previous_memory, input_tensor)
@@ -60,8 +61,6 @@ def tile_dynamicmemorycell_pa_s_kernel(
 
         load_rows(0, 0, 1)
         load_rows(1, 0, 1)
-        w_planes = keep.tile([P, PASSES, COLS], U8, align_bytes=64)
-        nc.vector.memset(w_planes[:].bitcast(I32), 0)
         scale_rows = fg_w_scales.bitcast(I32).rearrange("g q n -> q g n")
 
         def load_scales(r):
@@ -69,14 +68,12 @@ def tile_dynamicmemorycell_pa_s_kernel(
                 out=w_planes[r:P:32, :, :].bitcast(I32), in_=scale_rows[r : PACK * QUADRANTS : PACK, :, :]
             )
 
+        for r in range(PACK):
+            load_scales(r)
         load_rows(0, 1, ROW_TILES - 1)
         load_rows(1, 1, ROW_TILES - 1)
-        for r in range(PACK // 2):
-            load_scales(r)
         w_words = keep.tile([P, PASSES, 2 * COLS], U8, align_bytes=64)
         nc.sync.dma_start(out=w_words[:].bitcast(I32), in_=fg_w_words.bitcast(I32).rearrange("g p w -> p g w"))
-        for r in range(PACK // 2, PACK):
-            load_scales(r)
 
         ones = keep.tile([P, P], BF16)
         nc.vector.memset(ones[:], 1.0)
@@ -137,36 +134,36 @@ def tile_dynamicmemorycell_pa_s_kernel(
             nc.vector.tensor_tensor(out=result[:], in0=gate[i][:], in1=x_rows[(0, i)], op=MULT)
             nc.sync.dma_start(out=out_by_tile[:, i, :], in_=result[:])
 
-        def prepare(i):
-            for g in range(PASSES):
-                turn(i, g)
-                group(i, g)
+        def prepare(i, g):
+            turn(i, g)
+            group(i, g)
 
-        prepare(0)
-        prepare(1)
-        for g in range(PASSES):
-            quantise(0, g)
+        for i, g in [(0, 0), (0, 1), (1, 0), (2, 0)]:
+            prepare(i, g)
+        quantise(0, 0)
+        quantise(0, 1)
         bias_ps = psum_b.tile([P, COLS], BF16)
         nc.tensor.matmul(out=bias_ps[:], lhsT=ones[:], rhs=bias_rows[:], start=True, stop=True)
         bias_all = keep.tile([P, COLS], BF16)
         nc.vector.tensor_copy(out=bias_all[:], in_=bias_ps[:])
-        prepare(2)
-        for g in range(PASSES):
-            quantise(1, g)
+        quantise(1, 0)
+        quantise(2, 0)
+        prepare(3, 0)
+        quantise(3, 0)
+        for i in range(1, ROW_TILES):
+            prepare(i, 1)
+        quantise(1, 1)
         multiply(0)
-        prepare(3)
-        squash(0)
         multiply(1)
-        for g in range(PASSES):
-            quantise(2, g)
-        squash(1)
+        squash(0)
+        quantise(2, 1)
         multiply(2)
-        for g in range(PASSES):
-            quantise(3, g)
-        finish(0)
-        squash(2)
+        quantise(3, 1)
+        squash(1)
         multiply(3)
-        finish(1)
+        squash(2)
+        finish(0)
         squash(3)
+        finish(1)
         finish(2)
         finish(3)

@@ -21,7 +21,8 @@ PASSES = 2
 K_PASS = P * PACK
 ROW_TILES = ROWS // P
 QUADRANTS = 4
-WARM_UP = 3
+WARM_UP = 4
+KEEP_UP = 1
 
 FLOPS = 2 * ROWS * PASSES * K_PASS * COLS
 
@@ -32,7 +33,7 @@ def tile_dynamicmemorycell_pa_s_kernel(
     nc = tc.nc
     with tc.tile_pool(name="keep", bufs=1) as keep, tc.tile_pool(
         name="work", bufs=ROW_TILES * PASSES
-    ) as work, tc.psum_pool(name="psum_t", bufs=2 * PASSES) as psum_t, tc.psum_pool(
+    ) as work, tc.psum_pool(name="psum_t", bufs=3) as psum_t, tc.psum_pool(
         name="psum_z", bufs=ROW_TILES - 1
     ) as psum_z, tc.psum_pool(name="psum_b", bufs=1) as psum_b, tc.manual_schedule():
 
@@ -81,11 +82,15 @@ def tile_dynamicmemorycell_pa_s_kernel(
         nc.vector.memset(warm[:], 0.0)
         nc.scalar.activation(out=warm[:], in_=warm[:], func=SIGMOID)
 
-        idle_ps = psum_z.tile([P, P], F32, name="z")
-        for n in range(WARM_UP):
-            nc.tensor.matmul(
-                out=idle_ps[:], lhsT=warm_operand[:], rhs=warm_operand[:], start=(n == 0), stop=(n == WARM_UP - 1)
-            )
+        idle_ps = psum_b.tile([P, P], F32)
+
+        def keep_clock_up(count):
+            for n in range(count):
+                nc.tensor.matmul(
+                    out=idle_ps[:], lhsT=warm_operand[:], rhs=warm_operand[:], start=(n == 0), stop=(n == count - 1)
+                )
+
+        keep_clock_up(WARM_UP)
 
         turned, grouped, x_codes, x_planes, z, gate = {}, {}, {}, {}, {}, {}
 
@@ -138,27 +143,19 @@ def tile_dynamicmemorycell_pa_s_kernel(
             turn(i, g)
             group(i, g)
 
-        for i, g in [(0, 0), (0, 1), (1, 0), (2, 0)]:
-            prepare(i, g)
-        quantise(0, 0)
-        quantise(0, 1)
+        for pair in [((0, 0), (0, 1)), ((1, 0), (2, 0)), ((3, 0), (1, 1)), ((2, 1), (3, 1))]:
+            for half in pair:
+                prepare(*half)
+                quantise(*half)
+            keep_clock_up(KEEP_UP)
         bias_ps = psum_b.tile([P, COLS], BF16)
         nc.tensor.matmul(out=bias_ps[:], lhsT=ones[:], rhs=bias_rows[:], start=True, stop=True)
         bias_all = keep.tile([P, COLS], BF16)
         nc.vector.tensor_copy(out=bias_all[:], in_=bias_ps[:])
-        quantise(1, 0)
-        quantise(2, 0)
-        prepare(3, 0)
-        quantise(3, 0)
-        for i in range(1, ROW_TILES):
-            prepare(i, 1)
-        quantise(1, 1)
         multiply(0)
         multiply(1)
         squash(0)
-        quantise(2, 1)
         multiply(2)
-        quantise(3, 1)
         squash(1)
         multiply(3)
         squash(2)

@@ -33,14 +33,14 @@ def tile_dynamicmemorycell_pa_s_kernel(
     nc = tc.nc
     with tc.tile_pool(name="keep", bufs=1) as keep, tc.tile_pool(
         name="work", bufs=ROW_TILES * PASSES
-    ) as work, tc.psum_pool(name="psum_t", bufs=3) as psum_t, tc.psum_pool(
+    ) as work, tc.psum_pool(name="psum_t", bufs=2 * PASSES) as psum_t, tc.psum_pool(
         name="psum_z", bufs=ROW_TILES - 1
     ) as psum_z, tc.psum_pool(name="psum_b", bufs=1) as psum_b, tc.manual_schedule():
 
-        w_planes = keep.tile([P, PASSES, COLS], U8, align_bytes=64)
-        nc.vector.memset(w_planes[:].bitcast(I32), 0)
         warm_operand = keep.tile([P, P], F32)
         nc.vector.memset(warm_operand[:], 0.0)
+        w_planes = keep.tile([P, PASSES, COLS], U8, align_bytes=64)
+        nc.vector.memset(w_planes[:].bitcast(I32), 0)
         ident = keep.tile([P, P], F32)
         nc.vector.memset(ident[:], 0.0)
         make_identity(nc, ident[:], nomemset=True)
@@ -82,12 +82,13 @@ def tile_dynamicmemorycell_pa_s_kernel(
         nc.vector.memset(warm[:], 0.0)
         nc.scalar.activation(out=warm[:], in_=warm[:], func=SIGMOID)
 
-        idle_ps = psum_b.tile([P, P], F32)
+        spare_ps = psum_b.tile([P, COLS], F32)
+        idle_ps = spare_ps[:, :P]
 
         def keep_clock_up(count):
             for n in range(count):
                 nc.tensor.matmul(
-                    out=idle_ps[:], lhsT=warm_operand[:], rhs=warm_operand[:], start=(n == 0), stop=(n == count - 1)
+                    out=idle_ps, lhsT=warm_operand[:], rhs=warm_operand[:], start=(n == 0), stop=(n == count - 1)
                 )
 
         keep_clock_up(WARM_UP)
@@ -143,15 +144,24 @@ def tile_dynamicmemorycell_pa_s_kernel(
             turn(i, g)
             group(i, g)
 
-        for pair in [((0, 0), (0, 1)), ((1, 0), (2, 0)), ((3, 0), (1, 1)), ((2, 1), (3, 1))]:
-            for half in pair:
-                prepare(*half)
-                quantise(*half)
-            keep_clock_up(KEEP_UP)
-        bias_ps = psum_b.tile([P, COLS], BF16)
-        nc.tensor.matmul(out=bias_ps[:], lhsT=ones[:], rhs=bias_rows[:], start=True, stop=True)
+        for half in [(0, 0), (0, 1)]:
+            prepare(*half)
+            quantise(*half)
+        keep_clock_up(KEEP_UP)
+        for half in [(1, 0), (2, 0), (3, 0)]:
+            prepare(*half)
+            quantise(*half)
+        keep_clock_up(KEEP_UP)
+        for half in [(1, 1), (2, 1)]:
+            prepare(*half)
+        quantise(1, 1)
+        bias_ps = spare_ps[:, COLS // 2 :].bitcast(BF16)
+        nc.tensor.matmul(out=bias_ps, lhsT=ones[:], rhs=bias_rows[:], start=True, stop=True)
         bias_all = keep.tile([P, COLS], BF16)
-        nc.vector.tensor_copy(out=bias_all[:], in_=bias_ps[:])
+        nc.vector.tensor_copy(out=bias_all[:], in_=bias_ps)
+        quantise(2, 1)
+        prepare(3, 1)
+        quantise(3, 1)
         multiply(0)
         multiply(1)
         squash(0)

@@ -21,7 +21,7 @@ PASSES = 2
 K_PASS = P * PACK
 ROW_TILES = ROWS // P
 QUADRANTS = 4
-WARM_UP = 4
+WARM_UP = 3
 KEEP_UP = 1
 
 FLOPS = 2 * ROWS * PASSES * K_PASS * COLS
@@ -60,8 +60,9 @@ def tile_dynamicmemorycell_pa_s_kernel(
             for j in range(count):
                 x_rows[(g, first + j)] = loaded[:, j, :]
 
-        load_rows(0, 0, 1)
-        load_rows(1, 0, 1)
+        for first in range(0, ROW_TILES, 2):
+            for g in range(PASSES):
+                load_rows(g, first, 2)
         scale_rows = fg_w_scales.bitcast(I32).rearrange("g q n -> q g n")
 
         def load_scales(r):
@@ -71,8 +72,6 @@ def tile_dynamicmemorycell_pa_s_kernel(
 
         for r in range(PACK):
             load_scales(r)
-        load_rows(0, 1, ROW_TILES - 1)
-        load_rows(1, 1, ROW_TILES - 1)
         w_words = keep.tile([P, PASSES, 2 * COLS], U8, align_bytes=64)
         nc.sync.dma_start(out=w_words[:].bitcast(I32), in_=fg_w_words.bitcast(I32).rearrange("g p w -> p g w"))
 
@@ -144,24 +143,21 @@ def tile_dynamicmemorycell_pa_s_kernel(
             turn(i, g)
             group(i, g)
 
-        for half in [(0, 0), (0, 1)]:
-            prepare(*half)
-            quantise(*half)
-        keep_clock_up(KEEP_UP)
-        for half in [(1, 0), (2, 0), (3, 0)]:
-            prepare(*half)
-            quantise(*half)
-        keep_clock_up(KEEP_UP)
-        for half in [(1, 1), (2, 1)]:
-            prepare(*half)
-        quantise(1, 1)
+        for first, g in [(0, 0), (0, 1)]:
+            for i in (first, first + 1):
+                prepare(i, g)
+                quantise(i, g)
+            keep_clock_up(KEEP_UP)
+        for i in (2, 3):
+            prepare(i, 0)
+            quantise(i, 0)
         bias_ps = spare_ps[:, COLS // 2 :].bitcast(BF16)
         nc.tensor.matmul(out=bias_ps, lhsT=ones[:], rhs=bias_rows[:], start=True, stop=True)
         bias_all = keep.tile([P, COLS], BF16)
         nc.vector.tensor_copy(out=bias_all[:], in_=bias_ps)
-        quantise(2, 1)
-        prepare(3, 1)
-        quantise(3, 1)
+        for i in (2, 3):
+            prepare(i, 1)
+            quantise(i, 1)
         multiply(0)
         multiply(1)
         squash(0)

@@ -20,6 +20,9 @@ COLS = 512
 PASSES = 2
 K_PASS = P * PACK
 ROW_TILES = ROWS // P
+BANKS = 8
+SPLIT = 256
+GROUPS = (COLS - SPLIT) // P
 QUADRANTS = 4
 WARM_UP = 3
 KEEP_UP = 1
@@ -33,20 +36,20 @@ def tile_dynamicmemorycell_pa_s_kernel(
     nc = tc.nc
     with tc.tile_pool(name="keep", bufs=1) as keep, tc.tile_pool(
         name="work", bufs=ROW_TILES * PASSES
-    ) as work, tc.psum_pool(name="psum_t", bufs=2 * PASSES) as psum_t, tc.psum_pool(
-        name="psum_z", bufs=ROW_TILES - 1
-    ) as psum_z, tc.psum_pool(name="psum_b", bufs=1) as psum_b, tc.manual_schedule():
+    ) as work, tc.psum_pool(name="psum", bufs=BANKS - 1) as psum, tc.psum_pool(
+        name="psum_b", bufs=1
+    ) as psum_b, tc.manual_schedule():
 
-        warm_operand = keep.tile([P, P], F32)
-        nc.vector.memset(warm_operand[:], 0.0)
-        w_planes = keep.tile([P, PASSES, COLS], U8, align_bytes=64)
-        nc.vector.memset(w_planes[:].bitcast(I32), 0)
         ident = keep.tile([P, P], F32)
         nc.vector.memset(ident[:], 0.0)
         make_identity(nc, ident[:], nomemset=True)
+        warm_operand = keep.tile([P, P], F32)
+        nc.vector.memset(warm_operand[:], 0.0)
         bias_rows = keep.tile([P, COLS], BF16)
         nc.vector.memset(bias_rows[:].bitcast(I32), 0)
         nc.gpsimd.dma_start(out=bias_rows[0:1, :], in_=fg_b.rearrange("(o n) -> o n", o=1))
+        w_planes = keep.tile([P, PASSES, COLS], U8, align_bytes=64)
+        nc.vector.memset(w_planes[:].bitcast(I32), 0)
 
         by_tile = [
             source.rearrange("(p i) k -> p i k", i=ROW_TILES) for source in (previous_memory, input_tensor)
@@ -92,10 +95,11 @@ def tile_dynamicmemorycell_pa_s_kernel(
 
         keep_clock_up(WARM_UP)
 
-        turned, grouped, x_codes, x_planes, z, gate = {}, {}, {}, {}, {}, {}
+        turned, grouped, x_codes, x_planes = {}, {}, {}, {}
+        z_rows, z_cols, z_biased, gate_rows, gate_cols, gate_back, result = {}, {}, {}, {}, {}, {}, {}
 
         def turn(i, g):
-            turned[(i, g)] = psum_t.tile([P, PAIR, P], F32, name="turned")
+            turned[(i, g)] = psum.tile([P, PAIR, P], F32, name="bank")
             row_words = x_rows[(g, i)].bitcast(F32)
             for u in range(PAIR):
                 nc.tensor.transpose(turned[(i, g)][:, u, :], row_words[:, u : K_PASS // PAIR : PAIR], ident[:])
@@ -115,58 +119,109 @@ def tile_dynamicmemorycell_pa_s_kernel(
                 in_=grouped[(i, g)][:].rearrange("p b t -> p (b t)"),
             )
 
-        def multiply(i):
-            z[i] = psum_z.tile([P, COLS], F32, name="z")
-            for g in range(PASSES):
-                nc.tensor.matmul_mx(
-                    out=z[i][:],
-                    lhsT=x_codes[(i, g)][:].bitcast(FP8X4),
-                    lhsT_scale=x_planes[(i, g)][:],
-                    rhs=w_words[:, g, :].bitcast(FP4X4),
-                    rhs_scale=w_planes[:, g, :],
-                    start=(g == 0),
-                    stop=(g == PASSES - 1),
+        def multiply_rows(i):
+            z_rows[i] = psum.tile([P, SPLIT], F32, name="bank")
+            for n in range(0, SPLIT, P):
+                for g in range(PASSES):
+                    nc.tensor.matmul_mx(
+                        out=z_rows[i][:, n : n + P],
+                        lhsT=x_codes[(i, g)][:].bitcast(FP8X4),
+                        lhsT_scale=x_planes[(i, g)][:],
+                        rhs=w_words[:, g, 2 * n : 2 * (n + P)].bitcast(FP4X4),
+                        rhs_scale=w_planes[:, g, n : n + P],
+                        start=(g == 0),
+                        stop=(g == PASSES - 1),
+                    )
+
+        def multiply_cols(i):
+            z_cols[i] = psum.tile([P, GROUPS, P], F32, name="bank")
+            for j in range(GROUPS):
+                n = SPLIT + j * P
+                for g in range(PASSES):
+                    nc.tensor.matmul_mx(
+                        out=z_cols[i][:, j, :],
+                        lhsT=w_words[:, g, 2 * n : 2 * (n + P)].bitcast(FP4X4),
+                        lhsT_scale=w_planes[:, g, n : n + P],
+                        rhs=x_codes[(i, g)][:].bitcast(FP8X4),
+                        rhs_scale=x_planes[(i, g)][:],
+                        start=(g == 0),
+                        stop=(g == PASSES - 1),
+                    )
+
+        def add_bias(i):
+            z_biased[i] = work.tile([P, SPLIT], F32, name="z_biased")
+            nc.vector.tensor_tensor(out=z_biased[i][:], in0=z_rows[i][:], in1=bias_all[:], op=ADD)
+
+        def squash_rows(i):
+            gate_rows[i] = work.tile([P, SPLIT], F32, name="gate_rows")
+            nc.scalar.activation(out=gate_rows[i][:], in_=z_biased[i][:], func=SIGMOID)
+
+        def squash_cols(i):
+            gate_cols[i] = work.tile([P, GROUPS, P], F32, name="gate_cols")
+            for j in range(GROUPS):
+                nc.scalar.activation(
+                    out=gate_cols[i][:, j, :], in_=z_cols[i][:, j, :], func=SIGMOID, bias=bias_col[:, j : j + 1]
                 )
 
-        def squash(i):
-            z_biased = work.tile([P, COLS], F32)
-            nc.vector.tensor_tensor(out=z_biased[:], in0=z[i][:], in1=bias_all[:], op=ADD)
-            gate[i] = work.tile([P, COLS], F32, name="gate")
-            nc.scalar.activation(out=gate[i][:], in_=z_biased[:], func=SIGMOID)
+        def turn_back(i):
+            gate_back[i] = psum.tile([P, SPLIT], F32, name="bank")
+            for j in range(GROUPS):
+                nc.tensor.transpose(gate_back[i][:, j * P : (j + 1) * P], gate_cols[i][:, j, :], ident[:])
 
-        def finish(i):
-            result = work.tile([P, COLS], F32)
-            nc.vector.tensor_tensor(out=result[:], in0=gate[i][:], in1=x_rows[(0, i)], op=MULT)
-            nc.sync.dma_start(out=out_by_tile[:, i, :], in_=result[:])
+        def weigh_rows(i):
+            nc.vector.tensor_tensor(
+                out=result[i][:, :SPLIT], in0=gate_rows[i][:], in1=x_rows[(0, i)][:, :SPLIT], op=MULT
+            )
+
+        def weigh_cols(i):
+            result[i] = work.tile([P, COLS], F32, name="result")
+            nc.vector.tensor_tensor(
+                out=result[i][:, SPLIT:], in0=gate_back[i][:], in1=x_rows[(0, i)][:, SPLIT:], op=MULT
+            )
+
+        def store(i):
+            nc.sync.dma_start(out=out_by_tile[:, i, :], in_=result[i][:])
 
         def prepare(i, g):
             turn(i, g)
             group(i, g)
 
-        for first, g in [(0, 0), (0, 1)]:
-            for i in (first, first + 1):
-                prepare(i, g)
-                quantise(i, g)
-            keep_clock_up(KEEP_UP)
-        for i in (2, 3):
+        for i in (0, 1):
             prepare(i, 0)
             quantise(i, 0)
-        bias_ps = spare_ps[:, COLS // 2 :].bitcast(BF16)
-        nc.tensor.matmul(out=bias_ps, lhsT=ones[:], rhs=bias_rows[:], start=True, stop=True)
-        bias_all = keep.tile([P, COLS], BF16)
+        keep_clock_up(KEEP_UP)
+        for i in (0, 1):
+            prepare(i, 1)
+            quantise(i, 1)
+        keep_clock_up(KEEP_UP)
+        for i in (2, 3):
+            prepare(i, 0)
+        bias_ps = spare_ps[:, SPLIT : SPLIT + P].bitcast(BF16)
+        nc.tensor.matmul(out=bias_ps, lhsT=ones[:], rhs=bias_rows[:, :SPLIT], start=True, stop=True)
+        bias_col_ps = spare_ps[:, COLS - P :].rearrange("p (j n) -> p j n", j=GROUPS)
+        for j in range(GROUPS):
+            n = SPLIT + j * P
+            nc.tensor.matmul(
+                out=bias_col_ps[:, j, :2], lhsT=bias_rows[:, n : n + P], rhs=ones[:, :2], start=True, stop=True
+            )
+        bias_all = keep.tile([P, SPLIT], BF16)
         nc.vector.tensor_copy(out=bias_all[:], in_=bias_ps)
+        bias_col = keep.tile([P, GROUPS], F32)
+        nc.vector.tensor_copy(out=bias_col[:], in_=bias_col_ps[:, :, 0])
+        for i in (2, 3):
+            quantise(i, 0)
         for i in (2, 3):
             prepare(i, 1)
             quantise(i, 1)
-        multiply(0)
-        multiply(1)
-        squash(0)
-        multiply(2)
-        squash(1)
-        multiply(3)
-        squash(2)
-        finish(0)
-        squash(3)
-        finish(1)
-        finish(2)
-        finish(3)
+        for i in range(ROW_TILES + 1):
+            if i < ROW_TILES:
+                multiply_cols(i)
+                multiply_rows(i)
+                squash_cols(i)
+                add_bias(i)
+            if i > 0:
+                squash_rows(i - 1)
+                turn_back(i - 1)
+                weigh_cols(i - 1)
+                weigh_rows(i - 1)
+                store(i - 1)

import concourse.mybir as mybir
from concourse.masks import make_identity

F32 = mybir.dt.float32
BF16 = mybir.dt.bfloat16
I32 = mybir.dt.int32
U32 = mybir.dt.uint32
U8 = mybir.dt.uint8
FP8X4 = mybir.dt.float8_e4m3fn_x4
FP4X4 = mybir.dt.float4_e2m1fn_x4
ADD = mybir.AluOpType.add
MULT = mybir.AluOpType.mult
SIGMOID = mybir.ActivationFunctionType.Sigmoid

P = 128
PACK = 4
PAIR = 2
ROWS = 512
COLS = 512
PASSES = 2
K_PASS = P * PACK
ROW_TILES = ROWS // P
BANKS = 8
SPLIT = 256
GROUPS = (COLS - SPLIT) // P
QUADRANTS = 4
WARM_UP = 3
KEEP_UP = 1

FLOPS = 2 * ROWS * PASSES * K_PASS * COLS


def tile_dynamicmemorycell_pa_s_kernel(
    tc, input_tensor, previous_memory, fg_w_words, fg_w_scales, fg_b, out
):
    nc = tc.nc
    with tc.tile_pool(name="keep", bufs=1) as keep, tc.tile_pool(
        name="work", bufs=ROW_TILES * PASSES
    ) as work, tc.psum_pool(name="psum", bufs=BANKS - 1) as psum, tc.psum_pool(
        name="psum_b", bufs=1
    ) as psum_b, tc.manual_schedule():

        ident = keep.tile([P, P], F32)
        nc.vector.memset(ident[:], 0.0)
        make_identity(nc, ident[:], nomemset=True)
        warm_operand = keep.tile([P, P], F32)
        nc.vector.memset(warm_operand[:], 0.0)
        bias_rows = keep.tile([P, COLS], BF16)
        nc.vector.memset(bias_rows[:].bitcast(I32), 0)
        nc.gpsimd.dma_start(out=bias_rows[0:1, :], in_=fg_b.rearrange("(o n) -> o n", o=1))
        w_planes = keep.tile([P, PASSES, COLS], U8, align_bytes=64)
        nc.vector.memset(w_planes[:].bitcast(I32), 0)

        by_tile = [
            source.rearrange("(p i) k -> p i k", i=ROW_TILES) for source in (previous_memory, input_tensor)
        ]
        out_by_tile = out.rearrange("(p i) n -> p i n", i=ROW_TILES)
        x_rows = {}

        def load_rows(g, first, count):
            loaded = keep.tile([P, count, K_PASS], BF16, name="x_g%d_i%d" % (g, first))
            nc.sync.dma_start(out=loaded[:], in_=by_tile[g][:, first : first + count, :])
            for j in range(count):
                x_rows[(g, first + j)] = loaded[:, j, :]

        for first in range(0, ROW_TILES, 2):
            for g in range(PASSES):
                load_rows(g, first, 2)
        scale_rows = fg_w_scales.bitcast(I32).rearrange("g q n -> q g n")

        def load_scales(r):
            nc.sync.dma_start(
                out=w_planes[r:P:32, :, :].bitcast(I32), in_=scale_rows[r : PACK * QUADRANTS : PACK, :, :]
            )

        for r in range(PACK):
            load_scales(r)
        w_words = keep.tile([P, PASSES, 2 * COLS], U8, align_bytes=64)
        nc.sync.dma_start(out=w_words[:].bitcast(I32), in_=fg_w_words.bitcast(I32).rearrange("g p w -> p g w"))

        ones = keep.tile([P, P], BF16)
        nc.vector.memset(ones[:], 1.0)
        warm = keep.tile([P, 1], F32)
        nc.vector.memset(warm[:], 0.0)
        nc.scalar.activation(out=warm[:], in_=warm[:], func=SIGMOID)

        spare_ps = psum_b.tile([P, COLS], F32)
        idle_ps = spare_ps[:, :P]

        def keep_clock_up(count):
            for n in range(count):
                nc.tensor.matmul(
                    out=idle_ps, lhsT=warm_operand[:], rhs=warm_operand[:], start=(n == 0), stop=(n == count - 1)
                )

        keep_clock_up(WARM_UP)

        turned, grouped, x_codes, x_planes = {}, {}, {}, {}
        z_rows, z_cols, z_biased, gate_rows, gate_cols, gate_back, result = {}, {}, {}, {}, {}, {}, {}

        def turn(i, g):
            turned[(i, g)] = psum.tile([P, PAIR, P], F32, name="bank")
            row_words = x_rows[(g, i)].bitcast(F32)
            for u in range(PAIR):
                nc.tensor.transpose(turned[(i, g)][:, u, :], row_words[:, u : K_PASS // PAIR : PAIR], ident[:])

        def group(i, g):
            grouped[(i, g)] = work.tile([P, P, PACK], BF16, align_bytes=64, name="grouped")
            nc.scalar.copy(
                out=grouped[(i, g)][:].bitcast(F32), in_=turned[(i, g)][:].rearrange("p u b -> p b u")
            )

        def quantise(i, g):
            x_codes[(i, g)] = work.tile([P, P], U32, align_bytes=64, name="x_codes")
            x_planes[(i, g)] = work.tile([P, P], U8, align_bytes=64, name="x_planes")
            nc.vector.quantize_mx(
                out=x_codes[(i, g)][:].bitcast(FP8X4),
                scales=x_planes[(i, g)][:],
                in_=grouped[(i, g)][:].rearrange("p b t -> p (b t)"),
            )

        def multiply_rows(i):
            z_rows[i] = psum.tile([P, SPLIT], F32, name="bank")
            for n in range(0, SPLIT, P):
                for g in range(PASSES):
                    nc.tensor.matmul_mx(
                        out=z_rows[i][:, n : n + P],
                        lhsT=x_codes[(i, g)][:].bitcast(FP8X4),
                        lhsT_scale=x_planes[(i, g)][:],
                        rhs=w_words[:, g, 2 * n : 2 * (n + P)].bitcast(FP4X4),
                        rhs_scale=w_planes[:, g, n : n + P],
                        start=(g == 0),
                        stop=(g == PASSES - 1),
                    )

        def multiply_cols(i):
            z_cols[i] = psum.tile([P, GROUPS, P], F32, name="bank")
            for j in range(GROUPS):
                n = SPLIT + j * P
                for g in range(PASSES):
                    nc.tensor.matmul_mx(
                        out=z_cols[i][:, j, :],
                        lhsT=w_words[:, g, 2 * n : 2 * (n + P)].bitcast(FP4X4),
                        lhsT_scale=w_planes[:, g, n : n + P],
                        rhs=x_codes[(i, g)][:].bitcast(FP8X4),
                        rhs_scale=x_planes[(i, g)][:],
                        start=(g == 0),
                        stop=(g == PASSES - 1),
                    )

        def add_bias(i):
            z_biased[i] = work.tile([P, SPLIT], F32, name="z_biased")
            nc.vector.tensor_tensor(out=z_biased[i][:], in0=z_rows[i][:], in1=bias_all[:], op=ADD)

        def squash_rows(i):
            gate_rows[i] = work.tile([P, SPLIT], F32, name="gate_rows")
            nc.scalar.activation(out=gate_rows[i][:], in_=z_biased[i][:], func=SIGMOID)

        def squash_cols(i):
            gate_cols[i] = work.tile([P, GROUPS, P], F32, name="gate_cols")
            for j in range(GROUPS):
                nc.scalar.activation(
                    out=gate_cols[i][:, j, :], in_=z_cols[i][:, j, :], func=SIGMOID, bias=bias_col[:, j : j + 1]
                )

        def turn_back(i):
            gate_back[i] = psum.tile([P, SPLIT], F32, name="bank")
            for j in range(GROUPS):
                nc.tensor.transpose(gate_back[i][:, j * P : (j + 1) * P], gate_cols[i][:, j, :], ident[:])

        def weigh_rows(i):
            nc.vector.tensor_tensor(
                out=result[i][:, :SPLIT], in0=gate_rows[i][:], in1=x_rows[(0, i)][:, :SPLIT], op=MULT
            )

        def weigh_cols(i):
            result[i] = work.tile([P, COLS], F32, name="result")
            nc.vector.tensor_tensor(
                out=result[i][:, SPLIT:], in0=gate_back[i][:], in1=x_rows[(0, i)][:, SPLIT:], op=MULT
            )

        def store(i):
            nc.sync.dma_start(out=out_by_tile[:, i, :], in_=result[i][:])

        def prepare(i, g):
            turn(i, g)
            group(i, g)

        for i in (0, 1):
            prepare(i, 0)
            quantise(i, 0)
        keep_clock_up(KEEP_UP)
        for i in (0, 1):
            prepare(i, 1)
            quantise(i, 1)
        keep_clock_up(KEEP_UP)
        for i in (2, 3):
            prepare(i, 0)
        bias_ps = spare_ps[:, SPLIT : SPLIT + P].bitcast(BF16)
        nc.tensor.matmul(out=bias_ps, lhsT=ones[:], rhs=bias_rows[:, :SPLIT], start=True, stop=True)
        bias_col_ps = spare_ps[:, COLS - P :].rearrange("p (j n) -> p j n", j=GROUPS)
        for j in range(GROUPS):
            n = SPLIT + j * P
            nc.tensor.matmul(
                out=bias_col_ps[:, j, :2], lhsT=bias_rows[:, n : n + P], rhs=ones[:, :2], start=True, stop=True
            )
        bias_all = keep.tile([P, SPLIT], BF16)
        nc.vector.tensor_copy(out=bias_all[:], in_=bias_ps)
        bias_col = keep.tile([P, GROUPS], F32)
        nc.vector.tensor_copy(out=bias_col[:], in_=bias_col_ps[:, :, 0])
        for i in (2, 3):
            quantise(i, 0)
        for i in (2, 3):
            prepare(i, 1)
            quantise(i, 1)
        for i in range(ROW_TILES + 1):
            if i < ROW_TILES:
                multiply_cols(i)
                multiply_rows(i)
                squash_cols(i)
                add_bias(i)
            if i > 0:
                squash_rows(i - 1)
                turn_back(i - 1)
                weigh_cols(i - 1)
                weigh_rows(i - 1)
                store(i - 1)
